import numpy as np
import ml_dtypes


def mxq(x, axis, fmt="e4m3"):
    dtype, down = {"e4m3": (ml_dtypes.float8_e4m3fn, 7), "e5m2": (ml_dtypes.float8_e5m2, 14)}[fmt]
    v = np.moveaxis(np.asarray(x, np.float32).astype(ml_dtypes.bfloat16).astype(np.float64), axis, -1)
    blocks = v.reshape(v.shape[:-1] + (-1, 32))
    amax = np.abs(blocks).max(-1, keepdims=True)
    byte = np.maximum(np.where(amax > 0, np.frexp(amax)[1] - 1 + 127, 0) - down, 1)
    scale = np.exp2(byte - 127.0)
    codes = (blocks / scale).astype(np.float32).astype(dtype).astype(np.float64)
    return np.moveaxis((codes * scale).reshape(v.shape), -1, axis)


WIDE = False


def mx_kscale(k):
    if not WIDE:
        return np.ones(k)
    levels = np.array([10, -10, 5, -5, 0])
    a = np.random.permutation(np.resize(levels, k // 512 * 4)).reshape(k // 512, 4)
    idx = np.arange(k)
    return np.exp2(a[idx // 512, idx % 128 // 32])


BF16 = ml_dtypes.bfloat16


def bf(x):
    return np.asarray(x, np.float32).astype(BF16)


def f64(x):
    return np.asarray(x).astype(np.float64)


B, EMBED, HIDDEN, C, E = 512, 768, 2048, 32, 512
LS = 0.1


def setup_inputs():
    s, t = mx_kscale(HIDDEN), mx_kscale(E)
    x = np.random.standard_normal((B, HIDDEN))
    r = 0.6 + 0.8 * np.random.random((C, 1, 1))
    return {"h": bf(x / (1.0 + np.exp(-1.702 * x)) * s),
            "W3": bf(np.random.standard_normal((HIDDEN, E)) * 1.5 / np.sqrt(HIDDEN) / s[:, None] * t),
            "b3": bf(np.random.standard_normal(E) * 0.5 * t),
            "class_weight": bf(np.random.standard_normal((C, E, E)) * r * 0.14 / E / t[:, None]),
            "centroids": bf(np.random.standard_normal((C, E)) * 0.14 / np.sqrt(E))}


def reference(h, W3, b3, class_weight, centroids):
    z = (mxq(f64(h), 1, "e4m3") @ mxq(f64(W3), 0, "e4m3")) + f64(b3)
    weighted = (mxq(z, 1, "e4m3") @ mxq(f64(class_weight), 1, "e4m3")).transpose(1, 0, 2)
    diff = weighted - f64(centroids)[None, :, :]
    dist_sq = np.sum(diff * diff, axis=-1)
    log_kernel = -dist_sq / (2.0 * LS * LS)
    kernel_vals = np.exp(log_kernel)
    e = np.exp(log_kernel - log_kernel.max(-1, keepdims=True))
    probs = e / e.sum(-1, keepdims=True)
    uncertainty = 1.0 - kernel_vals.max(-1)
    return probs, probs[None], kernel_vals, uncertainty

@@ -1,0 +1,382 @@
+from contextlib import ExitStack
+
+import concourse.mybir as mybir
+from concourse.masks import make_identity
+
+F32 = mybir.dt.float32
+BF16 = mybir.dt.bfloat16
+U32 = mybir.dt.uint32
+U8 = mybir.dt.uint8
+FP8X4 = mybir.dt.float8_e4m3fn_x4
+ALU = mybir.AluOpType
+ACT = mybir.ActivationFunctionType
+AX = mybir.AxisListType
+
+P = 128
+B, HIDDEN, E, NCLS = 512, 2048, 512, 32
+LS = 0.1
+SCALE = -1.0 / (2.0 * LS * LS)
+FLOPS = 2 * B * HIDDEN * E + 2 * B * E * NCLS * E
+
+PIN = True
+N_A = 12
+N_JOBS = 4 * NCLS
+LA = 5
+GL = 1
+EL = 2
+LEAD = 8
+RAW_BUFS = 12
+GRP_BUFS = 4
+COD_BUFS = 10
+SQ_BUFS = 4
+DIF_BUFS = 4
+W_SPLIT = 64
+Z_SPLIT = 84
+
+
+def job_list():
+    raw_jobs = []
+    a = 0
+    c = 0
+    for j in range(N_JOBS):
+        if ((j + 1) * 4 * N_A) // N_JOBS > (j * 4 * N_A) // N_JOBS:
+            raw_jobs.append(("A", a // 4, a % 4))
+            a += 1
+        else:
+            raw_jobs.append(("C", c // 4, c % 4))
+            c += 1
+    number = {}
+    jobs = []
+    for form, r, part in raw_jobs:
+        if (form, r) not in number:
+            number[(form, r)] = len(number)
+        jobs.append((form, number[(form, r)], part))
+    return jobs
+
+
+def tile_duqhead_pa_kernel(tc, h, W3, b3, class_weight, centroids, out_0, out_1, out_2, out_3):
+    nc = tc.nc
+    jobs = job_list()
+    first_job = {}
+    form_of = {}
+    for j, (form, cls, part) in enumerate(jobs):
+        if cls not in first_job:
+            first_job[cls] = j
+            form_of[cls] = form
+    a_slot = {}
+    for cls in range(NCLS):
+        if form_of[cls] == "A":
+            a_slot[cls] = len(a_slot)
+    c_jobs = [j for j in range(N_JOBS) if jobs[j][0] == "C"]
+
+    with ExitStack() as ctx:
+        const = ctx.enter_context(tc.tile_pool(name="const", bufs=1))
+        raw = ctx.enter_context(tc.tile_pool(name="raw", bufs=RAW_BUFS))
+        grp = ctx.enter_context(tc.tile_pool(name="grp", bufs=GRP_BUFS))
+        cod = ctx.enter_context(tc.tile_pool(name="cod", bufs=COD_BUFS))
+        dif = ctx.enter_context(tc.tile_pool(name="dif", bufs=DIF_BUFS))
+        sqp = ctx.enter_context(tc.tile_pool(name="sqp", bufs=SQ_BUFS))
+        ps_c = ctx.enter_context(tc.psum_pool(name="ps_c", bufs=4))
+        ps_a = ctx.enter_context(tc.psum_pool(name="ps_a", bufs=3))
+        ps_acc = ctx.enter_context(tc.psum_pool(name="ps_acc", bufs=1))
+        if PIN:
+            ctx.enter_context(tc.manual_schedule())
+
+        b3r = const.tile([P, 4], BF16, name="b3r")
+        nc.scalar.dma_start(out=b3r[:], in_=b3.rearrange("(m t) -> m t", t=4))
+        cent128 = const.tile([P, P], BF16, name="cent128")
+        nc.scalar.dma_start(out=cent128[:], in_=centroids.rearrange("c (t p) -> (c t) p", p=P))
+        centb = const.tile([P, N_A * E], BF16, name="centb")
+
+        warm = const.tile([P, 2], F32, name="warm")
+        nc.vector.memset(warm[:], 0.0)
+        nc.scalar.activation(out=warm[:, 1:2], in_=warm[:, 0:1], func=ACT.Exp)
+        ident = const.tile([P, P], F32, name="ident")
+        make_identity(nc, ident[:])
+        onehot = const.tile([P, 33 * NCLS], F32, name="onehot")
+        nc.vector.memset(onehot[:], 0.0)
+        nc.vector.memset(onehot[:].rearrange("p (c k) -> p c k", k=33)[:, :, 0:1], 1.0)
+        dist_a = const.tile([P, 4 * NCLS], F32, name="dist_a")
+        nc.vector.memset(dist_a[:], 0.0)
+        unc = const.tile([P, P], F32, name="unc")
+        nc.vector.memset(unc[:], 0.0)
+
+        hcodes = const.tile([P, 4 * 512], U32, name="hcodes", align_bytes=64)
+        hscales = const.tile([P, 4 * 512], U8, name="hscales", align_bytes=64)
+        wcodes = const.tile([P, 4 * 512], U32, name="wcodes", align_bytes=64)
+        wscales = const.tile([P, 4 * 512], U8, name="wscales", align_bytes=64)
+        zcodes = const.tile([P, 512], U32, name="zcodes", align_bytes=64)
+        zscales = const.tile([P, 512], U8, name="zscales", align_bytes=64)
+        z_t = const.tile([P, 4 * 512], BF16, name="z_t")
+
+        h_v = h.rearrange("(t p) k -> p t k", t=4)
+        raw_h = []
+        raw_w = []
+        raw_c = {}
+        for g in range(4):
+            t = raw.tile([P, 2048], BF16, name="rawt", tag="rawt")
+            nc.sync.dma_start(out=t[:].rearrange("p (t k) -> p t k", t=4), in_=h_v[:, :, g * 512 : (g + 1) * 512])
+            raw_h.append(t)
+        for g in range(4):
+            t = raw.tile([P, 2048], BF16, name="rawt", tag="rawt")
+            nc.sync.dma_start(
+                out=t[:].rearrange("p (u e n) -> p u e n", u=2, e=2),
+                in_=W3[g * 512 : (g + 1) * 512, :].rearrange("(u q e) n -> q u e n", u=2, e=2),
+            )
+            raw_w.append(t)
+
+        def load_class(k):
+            if k >= NCLS:
+                return
+            if form_of[k] == "A":
+                s = a_slot[k]
+                nc.sync.dma_start(out=centb[:, s * E : (s + 1) * E], in_=centroids[k, :].partition_broadcast(P))
+            t = raw.tile([P, 2048], BF16, name="rawt", tag="rawt")
+            nc.sync.dma_start(out=t[:], in_=class_weight[k].rearrange("(p j) d -> p (j d)", j=4))
+            raw_c[k] = t
+
+        for k in range(RAW_BUFS - 8):
+            load_class(k)
+
+        b3f = const.tile([P, 4], F32, name="b3f")
+        nc.vector.tensor_copy(out=b3f[:], in_=b3r[:])
+        centn = const.tile([P, P], F32, name="centn")
+        nc.vector.tensor_scalar(out=centn[:], in0=cent128[:], scalar1=-1.0, scalar2=None, op0=ALU.mult)
+
+        hg = []
+
+        def quant(codes, scales, src):
+            nc.vector.quantize_mx(out=codes.bitcast(FP8X4), scales=scales, in_=src)
+
+        for g in range(4):
+            h32 = raw_h[g][:].bitcast(F32)
+            hgt = grp.tile([P, 2048], BF16, name="grpt", tag="grpt", align_bytes=64)
+            hg.append(hgt)
+            hg32 = hgt[:].bitcast(F32)
+            for half in range(2):
+                tp = ps_a.tile([P, 512], F32, name="bank_a", tag="bank_a")
+                for u in range(2):
+                    for bb in range(2):
+                        bt = 2 * half + bb
+                        nc.tensor.transpose(
+                            tp[:, u * 256 + bb * P : u * 256 + (bb + 1) * P],
+                            h32[:, bt * 256 + u * P : bt * 256 + (u + 1) * P],
+                            ident[:],
+                        )
+                dst = hg32[:, half * 512 : (half + 1) * 512].rearrange("p (b u) -> p b u", u=2)
+                src = tp[:].rearrange("p (u b) -> p b u", u=2)
+                if half == 0:
+                    nc.vector.tensor_copy(out=dst, in_=src)
+                else:
+                    nc.scalar.copy(out=dst, in_=src)
+            load_class(RAW_BUFS - 8 + g)
+            if g > 0:
+                quant(hcodes[:, (g - 1) * 512 : g * 512], hscales[:, (g - 1) * 512 : g * 512], hg[g - 1][:])
+
+        wg = []
+        zps = []
+
+        def regroup_w(g):
+            wgt = grp.tile([P, 2048], BF16, name="grpt", tag="grpt", align_bytes=64)
+            wg.append(wgt)
+            dst = wgt[:].rearrange("p (t m j) -> p m j t", t=4, j=4)
+            src = raw_w[g][:].rearrange("p (j m t) -> p m j t", j=4, t=4)
+            nc.vector.tensor_copy(out=dst[:, 0:W_SPLIT], in_=src[:, 0:W_SPLIT])
+            nc.scalar.copy(out=dst[:, W_SPLIT:P], in_=src[:, W_SPLIT:P])
+            load_class(RAW_BUFS - 4 + g)
+
+        def first_product(g):
+            quant(wcodes[:, g * 512 : (g + 1) * 512], wscales[:, g * 512 : (g + 1) * 512], wg[g][:])
+            for t in range(4):
+                if g == 0:
+                    zp = ps_c.tile([P, 512], F32, name="bank_c", tag="bank_c")
+                    zps.append(zp)
+                lo = g * 512 + t * P
+                nc.tensor.matmul_mx(
+                    out=zps[t][:],
+                    lhsT=wcodes[:, lo : lo + P].bitcast(FP8X4),
+                    lhsT_scale=wscales[:, lo : lo + P],
+                    rhs=hcodes[:, g * 512 : (g + 1) * 512].bitcast(FP8X4),
+                    rhs_scale=hscales[:, g * 512 : (g + 1) * 512],
+                    start=(g == 0),
+                    stop=(g == 3),
+                )
+
+        tpc = ps_a.tile([P, 512], F32, name="bank_a", tag="bank_a")
+        nc.tensor.transpose(tpc[:, 0:P], centn[:], ident[:])
+        regroup_w(0)
+        quant(hcodes[:, 3 * 512 : 4 * 512], hscales[:, 3 * 512 : 4 * 512], hg[3][:])
+        negcent = const.tile([P, P], F32, name="negcent")
+        nc.vector.tensor_copy(out=negcent[:], in_=tpc[:, 0:P])
+        for g in range(1, 4):
+            regroup_w(g)
+            first_product(g - 1)
+        first_product(3)
+
+        grp_c = {}
+        codes_c = {}
+        scales_c = {}
+
+        def regroup_class(k, engine):
+            gt = grp.tile([P, 2048], BF16, name="grpt", tag="grpt", align_bytes=64)
+            grp_c[k] = gt
+            dst = gt[:].rearrange("p (c i t) -> p c t i", i=4, t=4)
+            src = raw_c[k][:].rearrange("p (t c i) -> p c t i", t=4, i=4)
+            if engine == "V":
+                nc.vector.tensor_copy(out=dst, in_=src)
+            else:
+                nc.scalar.copy(out=dst, in_=src)
+            load_class(k + RAW_BUFS)
+
+        def quant_class(k):
+            ct = cod.tile([P, 512], U32, name="cwc", tag="cwc", align_bytes=64)
+            st = cod.tile([P, 512], U8, name="cws", tag="cws", align_bytes=64)
+            codes_c[k] = ct
+            scales_c[k] = st
+            quant(ct[:], st[:], grp_c[k][:])
+
+        regroup_class(0, "S")
+        regroup_class(1, "V")
+
+        for t in range(4):
+            dst = z_t[:, t * 512 : (t + 1) * 512]
+            if t < 2:
+                nc.scalar.activation(out=dst, in_=zps[t][:], func=ACT.Identity, bias=b3f[:, t : t + 1], scale=1.0)
+            else:
+                nc.vector.tensor_scalar(out=dst, in0=zps[t][:], scalar1=b3f[:, t : t + 1], scalar2=None, op0=ALU.add)
+        zg = grp.tile([P, 2048], BF16, name="grpt", tag="grpt", align_bytes=64)
+        dst = zg[:].rearrange("p (c i t) -> p c t i", i=4, t=4)
+        src = z_t[:].rearrange("p (t c i) -> p c t i", t=4, i=4)
+        nc.vector.tensor_copy(out=dst[:, 0:Z_SPLIT], in_=src[:, 0:Z_SPLIT])
+        nc.scalar.copy(out=dst[:, Z_SPLIT:P], in_=src[:, Z_SPLIT:P])
+        quant(zcodes[:], zscales[:], zg[:])
+        quant_class(0)
+        quant_class(1)
+
+        pieces = [("R", 2)]
+        for k in range(3, NCLS):
+            pieces.append(("R", k))
+            pieces.append(("Q", k - 1))
+        pieces.append(("Q", NCLS - 1))
+
+        def due(piece):
+            kind, k = piece
+            if kind == "R" and k > 2:
+                k = k - 1
+            return first_job[k] - LEAD
+
+        acc = ps_acc.tile([P, 4 * NCLS], F32, name="acc")
+        bank = {}
+        sq_t = {}
+        dif_t = {}
+
+        def second_product(j):
+            form, cls, part = jobs[j]
+            sl = slice(part * P, (part + 1) * P)
+            if form == "C":
+                ps = ps_c.tile([P, 512], F32, name="bank_c", tag="bank_c")
+                nc.tensor.matmul_mx(
+                    out=ps[:],
+                    lhsT=codes_c[cls][:, sl].bitcast(FP8X4),
+                    lhsT_scale=scales_c[cls][:, sl],
+                    rhs=zcodes[:].bitcast(FP8X4),
+                    rhs_scale=zscales[:],
+                    start=True,
+                    stop=True,
+                )
+            else:
+                ps = ps_a.tile([P, 512], F32, name="bank_a", tag="bank_a")
+                nc.tensor.matmul_mx(
+                    out=ps[:],
+                    lhsT=zcodes[:, sl].bitcast(FP8X4),
+                    lhsT_scale=zscales[:, sl],
+                    rhs=codes_c[cls][:].bitcast(FP8X4),
+                    rhs_scale=scales_c[cls][:],
+                    start=True,
+                    stop=True,
+                )
+            bank[j] = ps
+
+        def leave_psum(j):
+            form, cls, part = jobs[j]
+            if form == "C":
+                sq = sqp.tile([P, 512], F32, name="sq", tag="sq")
+                col = cls * 4 + part
+                nc.scalar.activation(out=sq[:], in_=bank[j][:], func=ACT.Square, bias=negcent[:, col : col + 1], scale=1.0)
+                sq_t[j] = sq
+            else:
+                df = dif.tile([P, 512], F32, name="df", tag="df")
+                s = a_slot[cls]
+                nc.vector.tensor_tensor(out=df[:], in0=bank[j][:], in1=centb[:, s * E : (s + 1) * E], op=ALU.subtract)
+                dif_t[j] = df
+
+        def sum_partitions(j):
+            form, cls, part = jobs[j]
+            for bt in range(4):
+                nc.tensor.matmul(
+                    out=acc[:, bt * NCLS : (bt + 1) * NCLS],
+                    lhsT=sq_t[j][:, bt * P : (bt + 1) * P],
+                    rhs=onehot[:, cls * NCLS : (cls + 1) * NCLS],
+                    start=(j == c_jobs[0] and bt == 0),
+                    stop=(j == c_jobs[-1] and bt == 3),
+                )
+
+        def sum_free(j):
+            form, cls, part = jobs[j]
+            col = part * NCLS + cls
+            nc.scalar.activation(out=dif_t[j][:], in_=dif_t[j][:], func=ACT.Square, accum_out=dist_a[:, col : col + 1])
+
+        for j in range(LA):
+            second_product(j)
+        done = 0
+        for j in range(N_JOBS + max(GL, EL)):
+            if j + LA < N_JOBS:
+                second_product(j + LA)
+            if j < N_JOBS:
+                leave_psum(j)
+            if 0 <= j - GL < N_JOBS and jobs[j - GL][0] == "C":
+                sum_partitions(j - GL)
+            if 0 <= j - EL < N_JOBS and jobs[j - EL][0] == "A":
+                sum_free(j - EL)
+            while done < len(pieces) and due(pieces[done]) <= j:
+                kind, k = pieces[done]
+                if kind == "R":
+                    regroup_class(k, "V")
+                else:
+                    quant_class(k)
+                done += 1
+
+        dist = const.tile([P, 4 * NCLS], F32, name="dist")
+        kv = const.tile([P, 4 * NCLS], F32, name="kv")
+        sh = const.tile([P, 4 * NCLS], F32, name="sh")
+        ex = const.tile([P, 4 * NCLS], F32, name="ex")
+        pr = const.tile([P, 4 * NCLS], F32, name="pr")
+        mn = const.tile([P, 4], F32, name="mn")
+        km = const.tile([P, 4], F32, name="km")
+        unc_t = const.tile([P, P], F32, name="unc_t")
+        ssum = const.tile([P, 4], F32, name="ssum")
+        rs = const.tile([P, 4], F32, name="rs")
+
+        def by_tile(x):
+            return x[:].rearrange("p (t c) -> p t c", t=4)
+
+        def spread(x):
+            return x[:].unsqueeze(2).to_broadcast([P, 4, NCLS])
+
+        nc.vector.tensor_tensor(out=dist[:], in0=acc[:], in1=dist_a[:], op=ALU.add)
+        nc.scalar.activation(out=kv[:], in_=dist[:], func=ACT.Exp, scale=SCALE)
+        nc.sync.dma_start(out=out_2.rearrange("(t p) c -> p t c", t=4), in_=by_tile(kv))
+        nc.vector.tensor_reduce(out=mn[:], in_=by_tile(dist), axis=AX.X, op=ALU.min)
+        nc.vector.tensor_tensor(out=by_tile(sh), in0=by_tile(dist), in1=spread(mn), op=ALU.subtract)
+        nc.scalar.activation(out=km[:], in_=mn[:], func=ACT.Exp, scale=SCALE)
+        nc.scalar.activation(out=ex[:], in_=sh[:], func=ACT.Exp, scale=SCALE)
+        nc.vector.tensor_scalar(out=unc[:, 0:4], in0=km[:], scalar1=-1.0, scalar2=1.0, op0=ALU.mult, op1=ALU.add)
+        unc_ps = ps_a.tile([P, 512], F32, name="bank_a", tag="bank_a")
+        nc.tensor.transpose(unc_ps[:, 0:P], unc[:], ident[:])
+        nc.vector.tensor_reduce(out=ssum[:], in_=by_tile(ex), axis=AX.X, op=ALU.add)
+        nc.scalar.copy(out=unc_t[0:32, :], in_=unc_ps[0:32, 0:P])
+        nc.sync.dma_start(out=out_3.rearrange("(t p) -> t p", t=4), in_=unc_t[0:4, :])
+        nc.vector.reciprocal(out=rs[:], in_=ssum[:])
+        nc.vector.tensor_tensor(out=by_tile(pr), in0=by_tile(ex), in1=spread(rs), op=ALU.mult)
+        nc.sync.dma_start(out=out_0.rearrange("(t p) c -> p t c", t=4), in_=by_tile(pr))
+        nc.sync.dma_start(out=out_1.rearrange("o (t p) c -> p (o t) c", t=4), in_=by_tile(pr))

@@ -18,17 +18,20 @@ LS = 0.1
 SCALE = -1.0 / (2.0 * LS * LS)
 FLOPS = 2 * B * HIDDEN * E + 2 * B * E * NCLS * E
 
-PIN = True
-N_A = 12
+N_A = 6
 N_JOBS = 4 * NCLS
-LA = 5
-GL = 1
-EL = 2
-LEAD = 8
+PHASE = 4
+BANKS_C = 4
+BANKS_A = 2
+BANKS_T = 2
+A_LAG = 3
+E_LAG = 4
+R_LAG = 5
+LEAD = 6
 RAW_BUFS = 12
 GRP_BUFS = 4
 COD_BUFS = 10
-SQ_BUFS = 4
+SQ_BUFS = 8
 DIF_BUFS = 4
 W_SPLIT = 64
 Z_SPLIT = 84
@@ -39,7 +42,7 @@ def job_list():
     a = 0
     c = 0
     for j in range(N_JOBS):
-        if ((j + 1) * 4 * N_A) // N_JOBS > (j * 4 * N_A) // N_JOBS:
+        if ((j + 1 + PHASE) * 4 * N_A) // N_JOBS > ((j + PHASE) * 4 * N_A) // N_JOBS:
             raw_jobs.append(("A", a // 4, a % 4))
             a += 1
         else:
@@ -68,6 +71,12 @@ def tile_duqhead_pa_kernel(tc, h, W3, b3, class_weight, centroids, out_0, out_1,
         if form_of[cls] == "A":
             a_slot[cls] = len(a_slot)
     c_jobs = [j for j in range(N_JOBS) if jobs[j][0] == "C"]
+    a_jobs = [j for j in range(N_JOBS) if jobs[j][0] == "A"]
+    issue = {}
+    for i, j in enumerate(c_jobs):
+        issue[j] = -1 if i < BANKS_C else c_jobs[i - BANKS_C]
+    for i, j in enumerate(a_jobs):
+        issue[j] = -1 if i < BANKS_A else a_jobs[i - BANKS_A] + A_LAG
 
     with ExitStack() as ctx:
         const = ctx.enter_context(tc.tile_pool(name="const", bufs=1))
@@ -76,11 +85,28 @@ def tile_duqhead_pa_kernel(tc, h, W3, b3, class_weight, centroids, out_0, out_1,
         cod = ctx.enter_context(tc.tile_pool(name="cod", bufs=COD_BUFS))
         dif = ctx.enter_context(tc.tile_pool(name="dif", bufs=DIF_BUFS))
         sqp = ctx.enter_context(tc.tile_pool(name="sqp", bufs=SQ_BUFS))
-        ps_c = ctx.enter_context(tc.psum_pool(name="ps_c", bufs=4))
-        ps_a = ctx.enter_context(tc.psum_pool(name="ps_a", bufs=3))
-        ps_acc = ctx.enter_context(tc.psum_pool(name="ps_acc", bufs=1))
-        if PIN:
-            ctx.enter_context(tc.manual_schedule())
+        ps_c = ctx.enter_context(tc.psum_pool(name="ps_c", bufs=BANKS_C))
+        ps_a = ctx.enter_context(tc.psum_pool(name="ps_a", bufs=BANKS_A))
+        ps_t = ctx.enter_context(tc.psum_pool(name="ps_t", bufs=BANKS_T))
+        ctx.enter_context(tc.manual_schedule())
+
+        def bank_c():
+            return ps_c.tile([P, 512], F32, name="bank_c", tag="bank_c")
+
+        def bank_a():
+            return ps_a.tile([P, 512], F32, name="bank_a", tag="bank_a")
+
+        def bank_t():
+            return ps_t.tile([P, 512], F32, name="bank_t", tag="bank_t")
+
+        def raw_tile():
+            return raw.tile([P, 2048], BF16, name="rawt", tag="rawt")
+
+        def grp_tile():
+            return grp.tile([P, 2048], BF16, name="grpt", tag="grpt", align_bytes=64)
+
+        def quant(codes, scales, src):
+            nc.vector.quantize_mx(out=codes.bitcast(FP8X4), scales=scales, in_=src)
 
         b3r = const.tile([P, 4], BF16, name="b3r")
         nc.scalar.dma_start(out=b3r[:], in_=b3.rearrange("(m t) -> m t", t=4))
@@ -93,9 +119,8 @@ def tile_duqhead_pa_kernel(tc, h, W3, b3, class_weight, centroids, out_0, out_1,
         nc.scalar.activation(out=warm[:, 1:2], in_=warm[:, 0:1], func=ACT.Exp)
         ident = const.tile([P, P], F32, name="ident")
         make_identity(nc, ident[:])
-        onehot = const.tile([P, 33 * NCLS], F32, name="onehot")
-        nc.vector.memset(onehot[:], 0.0)
-        nc.vector.memset(onehot[:].rearrange("p (c k) -> p c k", k=33)[:, :, 0:1], 1.0)
+        dist_c = const.tile([P, 4 * NCLS], F32, name="dist_c")
+        nc.vector.memset(dist_c[:], 0.0)
         dist_a = const.tile([P, 4 * NCLS], F32, name="dist_a")
         nc.vector.memset(dist_a[:], 0.0)
         unc = const.tile([P, P], F32, name="unc")
@@ -114,16 +139,16 @@ def tile_duqhead_pa_kernel(tc, h, W3, b3, class_weight, centroids, out_0, out_1,
         raw_w = []
         raw_c = {}
         for g in range(4):
-            t = raw.tile([P, 2048], BF16, name="rawt", tag="rawt")
-            nc.sync.dma_start(out=t[:].rearrange("p (t k) -> p t k", t=4), in_=h_v[:, :, g * 512 : (g + 1) * 512])
-            raw_h.append(t)
-        for g in range(4):
-            t = raw.tile([P, 2048], BF16, name="rawt", tag="rawt")
+            t = raw_tile()
             nc.sync.dma_start(
                 out=t[:].rearrange("p (u e n) -> p u e n", u=2, e=2),
                 in_=W3[g * 512 : (g + 1) * 512, :].rearrange("(u q e) n -> q u e n", u=2, e=2),
             )
             raw_w.append(t)
+        for g in range(4):
+            t = raw_tile()
+            nc.sync.dma_start(out=t[:].rearrange("p (t k) -> p t k", t=4), in_=h_v[:, :, g * 512 : (g + 1) * 512])
+            raw_h.append(t)
 
         def load_class(k):
             if k >= NCLS:
@@ -131,7 +156,7 @@ def tile_duqhead_pa_kernel(tc, h, W3, b3, class_weight, centroids, out_0, out_1,
             if form_of[k] == "A":
                 s = a_slot[k]
                 nc.sync.dma_start(out=centb[:, s * E : (s + 1) * E], in_=centroids[k, :].partition_broadcast(P))
-            t = raw.tile([P, 2048], BF16, name="rawt", tag="rawt")
+            t = raw_tile()
             nc.sync.dma_start(out=t[:], in_=class_weight[k].rearrange("(p j) d -> p (j d)", j=4))
             raw_c[k] = t
 
@@ -143,18 +168,52 @@ def tile_duqhead_pa_kernel(tc, h, W3, b3, class_weight, centroids, out_0, out_1,
         centn = const.tile([P, P], F32, name="centn")
         nc.vector.tensor_scalar(out=centn[:], in0=cent128[:], scalar1=-1.0, scalar2=None, op0=ALU.mult)
 
-        hg = []
+        wg = []
 
-        def quant(codes, scales, src):
-            nc.vector.quantize_mx(out=codes.bitcast(FP8X4), scales=scales, in_=src)
+        def regroup_w(g):
+            wgt = grp_tile()
+            wg.append(wgt)
+            dst = wgt[:].rearrange("p (t m j) -> p m j t", t=4, j=4)
+            src = raw_w[g][:].rearrange("p (j m t) -> p m j t", j=4, t=4)
+            nc.vector.tensor_copy(out=dst[:, 0:W_SPLIT], in_=src[:, 0:W_SPLIT])
+            nc.scalar.copy(out=dst[:, W_SPLIT:P], in_=src[:, W_SPLIT:P])
+            load_class(RAW_BUFS - 8 + g)
+
+        def quant_w(g):
+            quant(wcodes[:, g * 512 : (g + 1) * 512], wscales[:, g * 512 : (g + 1) * 512], wg[g][:])
+
+        regroup_w(0)
+        for g in range(1, 4):
+            regroup_w(g)
+            quant_w(g - 1)
+        quant_w(3)
+
+        hg = []
+        zps = []
+
+        def first_product(g):
+            quant(hcodes[:, g * 512 : (g + 1) * 512], hscales[:, g * 512 : (g + 1) * 512], hg[g][:])
+            for t in range(4):
+                if g == 0:
+                    zps.append(bank_c())
+                lo = g * 512 + t * P
+                nc.tensor.matmul_mx(
+                    out=zps[t][:],
+                    lhsT=wcodes[:, lo : lo + P].bitcast(FP8X4),
+                    lhsT_scale=wscales[:, lo : lo + P],
+                    rhs=hcodes[:, g * 512 : (g + 1) * 512].bitcast(FP8X4),
+                    rhs_scale=hscales[:, g * 512 : (g + 1) * 512],
+                    start=(g == 0),
+                    stop=(g == 3),
+                )
 
         for g in range(4):
             h32 = raw_h[g][:].bitcast(F32)
-            hgt = grp.tile([P, 2048], BF16, name="grpt", tag="grpt", align_bytes=64)
+            hgt = grp_tile()
             hg.append(hgt)
             hg32 = hgt[:].bitcast(F32)
             for half in range(2):
-                tp = ps_a.tile([P, 512], F32, name="bank_a", tag="bank_a")
+                tp = bank_a() if half == 0 else bank_t()
                 for u in range(2):
                     for bb in range(2):
                         bt = 2 * half + bb
@@ -169,56 +228,21 @@ def tile_duqhead_pa_kernel(tc, h, W3, b3, class_weight, centroids, out_0, out_1,
                     nc.vector.tensor_copy(out=dst, in_=src)
                 else:
                     nc.scalar.copy(out=dst, in_=src)
-            load_class(RAW_BUFS - 8 + g)
-            if g > 0:
-                quant(hcodes[:, (g - 1) * 512 : g * 512], hscales[:, (g - 1) * 512 : g * 512], hg[g - 1][:])
-
-        wg = []
-        zps = []
-
-        def regroup_w(g):
-            wgt = grp.tile([P, 2048], BF16, name="grpt", tag="grpt", align_bytes=64)
-            wg.append(wgt)
-            dst = wgt[:].rearrange("p (t m j) -> p m j t", t=4, j=4)
-            src = raw_w[g][:].rearrange("p (j m t) -> p m j t", j=4, t=4)
-            nc.vector.tensor_copy(out=dst[:, 0:W_SPLIT], in_=src[:, 0:W_SPLIT])
-            nc.scalar.copy(out=dst[:, W_SPLIT:P], in_=src[:, W_SPLIT:P])
             load_class(RAW_BUFS - 4 + g)
-
-        def first_product(g):
-            quant(wcodes[:, g * 512 : (g + 1) * 512], wscales[:, g * 512 : (g + 1) * 512], wg[g][:])
-            for t in range(4):
-                if g == 0:
-                    zp = ps_c.tile([P, 512], F32, name="bank_c", tag="bank_c")
-                    zps.append(zp)
-                lo = g * 512 + t * P
-                nc.tensor.matmul_mx(
-                    out=zps[t][:],
-                    lhsT=wcodes[:, lo : lo + P].bitcast(FP8X4),
-                    lhsT_scale=wscales[:, lo : lo + P],
-                    rhs=hcodes[:, g * 512 : (g + 1) * 512].bitcast(FP8X4),
-                    rhs_scale=hscales[:, g * 512 : (g + 1) * 512],
-                    start=(g == 0),
-                    stop=(g == 3),
-                )
-
-        tpc = ps_a.tile([P, 512], F32, name="bank_a", tag="bank_a")
+            if g > 0:
+                first_product(g - 1)
+        tpc = bank_a()
         nc.tensor.transpose(tpc[:, 0:P], centn[:], ident[:])
-        regroup_w(0)
-        quant(hcodes[:, 3 * 512 : 4 * 512], hscales[:, 3 * 512 : 4 * 512], hg[3][:])
+        first_product(3)
         negcent = const.tile([P, P], F32, name="negcent")
         nc.vector.tensor_copy(out=negcent[:], in_=tpc[:, 0:P])
-        for g in range(1, 4):
-            regroup_w(g)
-            first_product(g - 1)
-        first_product(3)
 
         grp_c = {}
         codes_c = {}
         scales_c = {}
 
         def regroup_class(k, engine):
-            gt = grp.tile([P, 2048], BF16, name="grpt", tag="grpt", align_bytes=64)
+            gt = grp_tile()
             grp_c[k] = gt
             dst = gt[:].rearrange("p (c i t) -> p c t i", i=4, t=4)
             src = raw_c[k][:].rearrange("p (t c i) -> p c t i", t=4, i=4)
@@ -244,7 +268,7 @@ def tile_duqhead_pa_kernel(tc, h, W3, b3, class_weight, centroids, out_0, out_1,
                 nc.scalar.activation(out=dst, in_=zps[t][:], func=ACT.Identity, bias=b3f[:, t : t + 1], scale=1.0)
             else:
                 nc.vector.tensor_scalar(out=dst, in0=zps[t][:], scalar1=b3f[:, t : t + 1], scalar2=None, op0=ALU.add)
-        zg = grp.tile([P, 2048], BF16, name="grpt", tag="grpt", align_bytes=64)
+        zg = grp_tile()
         dst = zg[:].rearrange("p (c i t) -> p c t i", i=4, t=4)
         src = z_t[:].rearrange("p (t c i) -> p c t i", t=4, i=4)
         nc.vector.tensor_copy(out=dst[:, 0:Z_SPLIT], in_=src[:, 0:Z_SPLIT])
@@ -263,9 +287,9 @@ def tile_duqhead_pa_kernel(tc, h, W3, b3, class_weight, centroids, out_0, out_1,
             kind, k = piece
             if kind == "R" and k > 2:
                 k = k - 1
-            return first_job[k] - LEAD
+            return issue[first_job[k]] - LEAD
 
-        acc = ps_acc.tile([P, 4 * NCLS], F32, name="acc")
+        acc_t = {}
         bank = {}
         sq_t = {}
         dif_t = {}
@@ -274,7 +298,7 @@ def tile_duqhead_pa_kernel(tc, h, W3, b3, class_weight, centroids, out_0, out_1,
             form, cls, part = jobs[j]
             sl = slice(part * P, (part + 1) * P)
             if form == "C":
-                ps = ps_c.tile([P, 512], F32, name="bank_c", tag="bank_c")
+                ps = bank_c()
                 nc.tensor.matmul_mx(
                     out=ps[:],
                     lhsT=codes_c[cls][:, sl].bitcast(FP8X4),
@@ -285,7 +309,7 @@ def tile_duqhead_pa_kernel(tc, h, W3, b3, class_weight, centroids, out_0, out_1,
                     stop=True,
                 )
             else:
-                ps = ps_a.tile([P, 512], F32, name="bank_a", tag="bank_a")
+                ps = bank_a()
                 nc.tensor.matmul_mx(
                     out=ps[:],
                     lhsT=zcodes[:, sl].bitcast(FP8X4),
@@ -310,34 +334,44 @@ def tile_duqhead_pa_kernel(tc, h, W3, b3, class_weight, centroids, out_0, out_1,
                 nc.vector.tensor_tensor(out=df[:], in0=bank[j][:], in1=centb[:, s * E : (s + 1) * E], op=ALU.subtract)
                 dif_t[j] = df
 
-        def sum_partitions(j):
+        def sum_tiles(j):
             form, cls, part = jobs[j]
+            mine = [i for i in c_jobs if jobs[i][1] == cls]
+            acc = bank_t()
             for bt in range(4):
-                nc.tensor.matmul(
-                    out=acc[:, bt * NCLS : (bt + 1) * NCLS],
-                    lhsT=sq_t[j][:, bt * P : (bt + 1) * P],
-                    rhs=onehot[:, cls * NCLS : (cls + 1) * NCLS],
-                    start=(j == c_jobs[0] and bt == 0),
-                    stop=(j == c_jobs[-1] and bt == 3),
-                )
+                for dt in range(4):
+                    nc.tensor.matmul(
+                        out=acc[:, bt * P : (bt + 1) * P],
+                        lhsT=sq_t[mine[dt]][:, bt * P : (bt + 1) * P],
+                        rhs=ident[:],
+                        is_transpose=True,
+                        start=(dt == 0),
+                        stop=(dt == 3),
+                    )
+            acc_t[cls] = acc
+
+        def sum_rest(j):
+            form, cls, part = jobs[j]
+            nc.vector.tensor_reduce(
+                out=dist_c[:].rearrange("p (t c) -> p t c", t=4)[:, :, cls],
+                in_=acc_t[cls][:].rearrange("p (t q) -> p t q", t=4),
+                axis=AX.X,
+                op=ALU.add,
+            )
 
         def sum_free(j):
             form, cls, part = jobs[j]
             col = part * NCLS + cls
             nc.scalar.activation(out=dif_t[j][:], in_=dif_t[j][:], func=ACT.Square, accum_out=dist_a[:, col : col + 1])
 
-        for j in range(LA):
-            second_product(j)
+        def closes_class(j):
+            return 0 <= j < N_JOBS and jobs[j][0] == "C" and jobs[j][2] == 3
+
+        for j in range(N_JOBS):
+            if issue[j] == -1:
+                second_product(j)
         done = 0
-        for j in range(N_JOBS + max(GL, EL)):
-            if j + LA < N_JOBS:
-                second_product(j + LA)
-            if j < N_JOBS:
-                leave_psum(j)
-            if 0 <= j - GL < N_JOBS and jobs[j - GL][0] == "C":
-                sum_partitions(j - GL)
-            if 0 <= j - EL < N_JOBS and jobs[j - EL][0] == "A":
-                sum_free(j - EL)
+        for j in range(N_JOBS + max(R_LAG, E_LAG, A_LAG) + 1):
             while done < len(pieces) and due(pieces[done]) <= j:
                 kind, k = pieces[done]
                 if kind == "R":
@@ -345,6 +379,17 @@ def tile_duqhead_pa_kernel(tc, h, W3, b3, class_weight, centroids, out_0, out_1,
                 else:
                     quant_class(k)
                 done += 1
+            if j < N_JOBS:
+                leave_psum(j)
+            for i in range(N_JOBS):
+                if issue[i] == j:
+                    second_product(i)
+            if closes_class(j):
+                sum_tiles(j)
+            if closes_class(j - R_LAG):
+                sum_rest(j - R_LAG)
+            if 0 <= j - E_LAG < N_JOBS and jobs[j - E_LAG][0] == "A":
+                sum_free(j - E_LAG)
 
         dist = const.tile([P, 4 * NCLS], F32, name="dist")
         kv = const.tile([P, 4 * NCLS], F32, name="kv")
@@ -363,7 +408,7 @@ def tile_duqhead_pa_kernel(tc, h, W3, b3, class_weight, centroids, out_0, out_1,
         def spread(x):
             return x[:].unsqueeze(2).to_broadcast([P, 4, NCLS])
 
-        nc.vector.tensor_tensor(out=dist[:], in0=acc[:], in1=dist_a[:], op=ALU.add)
+        nc.vector.tensor_tensor(out=dist[:], in0=dist_c[:], in1=dist_a[:], op=ALU.add)
         nc.scalar.activation(out=kv[:], in_=dist[:], func=ACT.Exp, scale=SCALE)
         nc.sync.dma_start(out=out_2.rearrange("(t p) c -> p t c", t=4), in_=by_tile(kv))
         nc.vector.tensor_reduce(out=mn[:], in_=by_tile(dist), axis=AX.X, op=ALU.min)
@@ -371,7 +416,7 @@ def tile_duqhead_pa_kernel(tc, h, W3, b3, class_weight, centroids, out_0, out_1,
         nc.scalar.activation(out=km[:], in_=mn[:], func=ACT.Exp, scale=SCALE)
         nc.scalar.activation(out=ex[:], in_=sh[:], func=ACT.Exp, scale=SCALE)
         nc.vector.tensor_scalar(out=unc[:, 0:4], in0=km[:], scalar1=-1.0, scalar2=1.0, op0=ALU.mult, op1=ALU.add)
-        unc_ps = ps_a.tile([P, 512], F32, name="bank_a", tag="bank_a")
+        unc_ps = bank_a()
         nc.tensor.transpose(unc_ps[:, 0:P], unc[:], ident[:])
         nc.vector.tensor_reduce(out=ssum[:], in_=by_tile(ex), axis=AX.X, op=ALU.add)
         nc.scalar.copy(out=unc_t[0:32, :], in_=unc_ps[0:32, 0:P])

@@ -18,9 +18,9 @@ LS = 0.1
 SCALE = -1.0 / (2.0 * LS * LS)
 FLOPS = 2 * B * HIDDEN * E + 2 * B * E * NCLS * E
 
-N_A = 6
+N_A = 9
 N_JOBS = 4 * NCLS
-PHASE = 4
+PHASE = 2
 BANKS_C = 4
 BANKS_A = 2
 BANKS_T = 2

@@ -18,86 +18,42 @@ LS = 0.1
 SCALE = -1.0 / (2.0 * LS * LS)
 FLOPS = 2 * B * HIDDEN * E + 2 * B * E * NCLS * E
 
-N_A = 9
 N_JOBS = 4 * NCLS
-PHASE = 2
 BANKS_C = 4
-BANKS_A = 2
 BANKS_T = 2
-A_LAG = 3
-E_LAG = 4
-R_LAG = 5
-LEAD = 6
+BANKS_H = 2
+R_LAG = 3
+LEAD = 4
 RAW_BUFS = 12
 GRP_BUFS = 4
-COD_BUFS = 10
+COD_BUFS = 8
 SQ_BUFS = 8
-DIF_BUFS = 4
 W_SPLIT = 64
 Z_SPLIT = 84
 
 
-def job_list():
-    raw_jobs = []
-    a = 0
-    c = 0
-    for j in range(N_JOBS):
-        if ((j + 1 + PHASE) * 4 * N_A) // N_JOBS > ((j + PHASE) * 4 * N_A) // N_JOBS:
-            raw_jobs.append(("A", a // 4, a % 4))
-            a += 1
-        else:
-            raw_jobs.append(("C", c // 4, c % 4))
-            c += 1
-    number = {}
-    jobs = []
-    for form, r, part in raw_jobs:
-        if (form, r) not in number:
-            number[(form, r)] = len(number)
-        jobs.append((form, number[(form, r)], part))
-    return jobs
-
-
 def tile_duqhead_pa_kernel(tc, h, W3, b3, class_weight, centroids, out_0, out_1, out_2, out_3):
     nc = tc.nc
-    jobs = job_list()
-    first_job = {}
-    form_of = {}
-    for j, (form, cls, part) in enumerate(jobs):
-        if cls not in first_job:
-            first_job[cls] = j
-            form_of[cls] = form
-    a_slot = {}
-    for cls in range(NCLS):
-        if form_of[cls] == "A":
-            a_slot[cls] = len(a_slot)
-    c_jobs = [j for j in range(N_JOBS) if jobs[j][0] == "C"]
-    a_jobs = [j for j in range(N_JOBS) if jobs[j][0] == "A"]
-    issue = {}
-    for i, j in enumerate(c_jobs):
-        issue[j] = -1 if i < BANKS_C else c_jobs[i - BANKS_C]
-    for i, j in enumerate(a_jobs):
-        issue[j] = -1 if i < BANKS_A else a_jobs[i - BANKS_A] + A_LAG
 
     with ExitStack() as ctx:
         const = ctx.enter_context(tc.tile_pool(name="const", bufs=1))
         raw = ctx.enter_context(tc.tile_pool(name="raw", bufs=RAW_BUFS))
         grp = ctx.enter_context(tc.tile_pool(name="grp", bufs=GRP_BUFS))
         cod = ctx.enter_context(tc.tile_pool(name="cod", bufs=COD_BUFS))
-        dif = ctx.enter_context(tc.tile_pool(name="dif", bufs=DIF_BUFS))
         sqp = ctx.enter_context(tc.tile_pool(name="sqp", bufs=SQ_BUFS))
         ps_c = ctx.enter_context(tc.psum_pool(name="ps_c", bufs=BANKS_C))
-        ps_a = ctx.enter_context(tc.psum_pool(name="ps_a", bufs=BANKS_A))
         ps_t = ctx.enter_context(tc.psum_pool(name="ps_t", bufs=BANKS_T))
+        ps_h = ctx.enter_context(tc.psum_pool(name="ps_h", bufs=BANKS_H))
         ctx.enter_context(tc.manual_schedule())
 
         def bank_c():
             return ps_c.tile([P, 512], F32, name="bank_c", tag="bank_c")
 
-        def bank_a():
-            return ps_a.tile([P, 512], F32, name="bank_a", tag="bank_a")
-
         def bank_t():
             return ps_t.tile([P, 512], F32, name="bank_t", tag="bank_t")
+
+        def bank_h():
+            return ps_h.tile([P, 512], F32, name="bank_h", tag="bank_h")
 
         def raw_tile():
             return raw.tile([P, 2048], BF16, name="rawt", tag="rawt")
@@ -112,17 +68,12 @@ def tile_duqhead_pa_kernel(tc, h, W3, b3, class_weight, centroids, out_0, out_1,
         nc.scalar.dma_start(out=b3r[:], in_=b3.rearrange("(m t) -> m t", t=4))
         cent128 = const.tile([P, P], BF16, name="cent128")
         nc.scalar.dma_start(out=cent128[:], in_=centroids.rearrange("c (t p) -> (c t) p", p=P))
-        centb = const.tile([P, N_A * E], BF16, name="centb")
 
         warm = const.tile([P, 2], F32, name="warm")
         nc.vector.memset(warm[:], 0.0)
         nc.scalar.activation(out=warm[:, 1:2], in_=warm[:, 0:1], func=ACT.Exp)
         ident = const.tile([P, P], F32, name="ident")
         make_identity(nc, ident[:])
-        dist_c = const.tile([P, 4 * NCLS], F32, name="dist_c")
-        nc.vector.memset(dist_c[:], 0.0)
-        dist_a = const.tile([P, 4 * NCLS], F32, name="dist_a")
-        nc.vector.memset(dist_a[:], 0.0)
         unc = const.tile([P, P], F32, name="unc")
         nc.vector.memset(unc[:], 0.0)
 
@@ -133,6 +84,7 @@ def tile_duqhead_pa_kernel(tc, h, W3, b3, class_weight, centroids, out_0, out_1,
         zcodes = const.tile([P, 512], U32, name="zcodes", align_bytes=64)
         zscales = const.tile([P, 512], U8, name="zscales", align_bytes=64)
         z_t = const.tile([P, 4 * 512], BF16, name="z_t")
+        dist = const.tile([P, 4 * NCLS], F32, name="dist")
 
         h_v = h.rearrange("(t p) k -> p t k", t=4)
         raw_h = []
@@ -151,14 +103,10 @@ def tile_duqhead_pa_kernel(tc, h, W3, b3, class_weight, centroids, out_0, out_1,
             raw_h.append(t)
 
         def load_class(k):
-            if k >= NCLS:
-                return
-            if form_of[k] == "A":
-                s = a_slot[k]
-                nc.sync.dma_start(out=centb[:, s * E : (s + 1) * E], in_=centroids[k, :].partition_broadcast(P))
-            t = raw_tile()
-            nc.sync.dma_start(out=t[:], in_=class_weight[k].rearrange("(p j) d -> p (j d)", j=4))
-            raw_c[k] = t
+            if k < NCLS:
+                t = raw_tile()
+                nc.sync.dma_start(out=t[:], in_=class_weight[k].rearrange("(p j) d -> p (j d)", j=4))
+                raw_c[k] = t
 
         for k in range(RAW_BUFS - 8):
             load_class(k)
@@ -213,7 +161,7 @@ def tile_duqhead_pa_kernel(tc, h, W3, b3, class_weight, centroids, out_0, out_1,
             hg.append(hgt)
             hg32 = hgt[:].bitcast(F32)
             for half in range(2):
-                tp = bank_a() if half == 0 else bank_t()
+                tp = bank_h() if half == 0 else bank_t()
                 for u in range(2):
                     for bb in range(2):
                         bt = 2 * half + bb
@@ -224,32 +172,27 @@ def tile_duqhead_pa_kernel(tc, h, W3, b3, class_weight, centroids, out_0, out_1,
                         )
                 dst = hg32[:, half * 512 : (half + 1) * 512].rearrange("p (b u) -> p b u", u=2)
                 src = tp[:].rearrange("p (u b) -> p b u", u=2)
-                if half == 0:
+                if half == 0 and g == 3:
                     nc.vector.tensor_copy(out=dst, in_=src)
                 else:
                     nc.scalar.copy(out=dst, in_=src)
             load_class(RAW_BUFS - 4 + g)
             if g > 0:
                 first_product(g - 1)
-        tpc = bank_a()
+        tpc = bank_h()
         nc.tensor.transpose(tpc[:, 0:P], centn[:], ident[:])
         first_product(3)
-        negcent = const.tile([P, P], F32, name="negcent")
-        nc.vector.tensor_copy(out=negcent[:], in_=tpc[:, 0:P])
 
         grp_c = {}
         codes_c = {}
         scales_c = {}
 
-        def regroup_class(k, engine):
+        def regroup_class(k):
             gt = grp_tile()
             grp_c[k] = gt
             dst = gt[:].rearrange("p (c i t) -> p c t i", i=4, t=4)
             src = raw_c[k][:].rearrange("p (t c i) -> p c t i", t=4, i=4)
-            if engine == "V":
-                nc.vector.tensor_copy(out=dst, in_=src)
-            else:
-                nc.scalar.copy(out=dst, in_=src)
+            nc.vector.tensor_copy(out=dst, in_=src)
             load_class(k + RAW_BUFS)
 
         def quant_class(k):
@@ -259,12 +202,14 @@ def tile_duqhead_pa_kernel(tc, h, W3, b3, class_weight, centroids, out_0, out_1,
             scales_c[k] = st
             quant(ct[:], st[:], grp_c[k][:])
 
-        regroup_class(0, "S")
-        regroup_class(1, "V")
+        regroup_class(0)
+        negcent = const.tile([P, P], F32, name="negcent")
+        nc.vector.tensor_copy(out=negcent[:], in_=tpc[:, 0:P])
+        quant_class(0)
 
         for t in range(4):
             dst = z_t[:, t * 512 : (t + 1) * 512]
-            if t < 2:
+            if t < 3:
                 nc.scalar.activation(out=dst, in_=zps[t][:], func=ACT.Identity, bias=b3f[:, t : t + 1], scale=1.0)
             else:
                 nc.vector.tensor_scalar(out=dst, in0=zps[t][:], scalar1=b3f[:, t : t + 1], scalar2=None, op0=ALU.add)
@@ -274,10 +219,8 @@ def tile_duqhead_pa_kernel(tc, h, W3, b3, class_weight, centroids, out_0, out_1,
         nc.vector.tensor_copy(out=dst[:, 0:Z_SPLIT], in_=src[:, 0:Z_SPLIT])
         nc.scalar.copy(out=dst[:, Z_SPLIT:P], in_=src[:, Z_SPLIT:P])
         quant(zcodes[:], zscales[:], zg[:])
-        quant_class(0)
-        quant_class(1)
 
-        pieces = [("R", 2)]
+        pieces = [("R", 1), ("Q", 1), ("R", 2)]
         for k in range(3, NCLS):
             pieces.append(("R", k))
             pieces.append(("Q", k - 1))
@@ -287,111 +230,82 @@ def tile_duqhead_pa_kernel(tc, h, W3, b3, class_weight, centroids, out_0, out_1,
             kind, k = piece
             if kind == "R" and k > 2:
                 k = k - 1
-            return issue[first_job[k]] - LEAD
+            return 4 * k - BANKS_C - LEAD
 
         acc_t = {}
         bank = {}
         sq_t = {}
-        dif_t = {}
 
         def second_product(j):
-            form, cls, part = jobs[j]
-            sl = slice(part * P, (part + 1) * P)
-            if form == "C":
-                ps = bank_c()
-                nc.tensor.matmul_mx(
-                    out=ps[:],
-                    lhsT=codes_c[cls][:, sl].bitcast(FP8X4),
-                    lhsT_scale=scales_c[cls][:, sl],
-                    rhs=zcodes[:].bitcast(FP8X4),
-                    rhs_scale=zscales[:],
-                    start=True,
-                    stop=True,
-                )
-            else:
-                ps = bank_a()
-                nc.tensor.matmul_mx(
-                    out=ps[:],
-                    lhsT=zcodes[:, sl].bitcast(FP8X4),
-                    lhsT_scale=zscales[:, sl],
-                    rhs=codes_c[cls][:].bitcast(FP8X4),
-                    rhs_scale=scales_c[cls][:],
-                    start=True,
-                    stop=True,
-                )
+            cls = j // 4
+            sl = slice((j % 4) * P, (j % 4 + 1) * P)
+            ps = bank_c()
+            nc.tensor.matmul_mx(
+                out=ps[:],
+                lhsT=codes_c[cls][:, sl].bitcast(FP8X4),
+                lhsT_scale=scales_c[cls][:, sl],
+                rhs=zcodes[:].bitcast(FP8X4),
+                rhs_scale=zscales[:],
+                start=True,
+                stop=True,
+            )
             bank[j] = ps
 
-        def leave_psum(j):
-            form, cls, part = jobs[j]
-            if form == "C":
-                sq = sqp.tile([P, 512], F32, name="sq", tag="sq")
-                col = cls * 4 + part
-                nc.scalar.activation(out=sq[:], in_=bank[j][:], func=ACT.Square, bias=negcent[:, col : col + 1], scale=1.0)
-                sq_t[j] = sq
-            else:
-                df = dif.tile([P, 512], F32, name="df", tag="df")
-                s = a_slot[cls]
-                nc.vector.tensor_tensor(out=df[:], in0=bank[j][:], in1=centb[:, s * E : (s + 1) * E], op=ALU.subtract)
-                dif_t[j] = df
+        def square(j):
+            sq = sqp.tile([P, 512], F32, name="sq", tag="sq")
+            nc.scalar.activation(out=sq[:], in_=bank[j][:], func=ACT.Square, bias=negcent[:, j : j + 1], scale=1.0)
+            sq_t[j] = sq
 
-        def sum_tiles(j):
-            form, cls, part = jobs[j]
-            mine = [i for i in c_jobs if jobs[i][1] == cls]
-            acc = bank_t()
-            for bt in range(4):
-                for dt in range(4):
-                    nc.tensor.matmul(
-                        out=acc[:, bt * P : (bt + 1) * P],
-                        lhsT=sq_t[mine[dt]][:, bt * P : (bt + 1) * P],
-                        rhs=ident[:],
-                        is_transpose=True,
-                        start=(dt == 0),
-                        stop=(dt == 3),
-                    )
-            acc_t[cls] = acc
+        def add_transposed(cls, dt, bt, start, stop):
+            nc.tensor.matmul(
+                out=acc_t[cls][:, bt * P : (bt + 1) * P],
+                lhsT=sq_t[4 * cls + dt][:, bt * P : (bt + 1) * P],
+                rhs=ident[:],
+                is_transpose=True,
+                start=start,
+                stop=stop,
+            )
 
-        def sum_rest(j):
-            form, cls, part = jobs[j]
+        def sum_rest(cls):
             nc.vector.tensor_reduce(
-                out=dist_c[:].rearrange("p (t c) -> p t c", t=4)[:, :, cls],
+                out=dist[:].rearrange("p (t c) -> p t c", t=4)[:, :, cls],
                 in_=acc_t[cls][:].rearrange("p (t q) -> p t q", t=4),
                 axis=AX.X,
                 op=ALU.add,
             )
 
-        def sum_free(j):
-            form, cls, part = jobs[j]
-            col = part * NCLS + cls
-            nc.scalar.activation(out=dif_t[j][:], in_=dif_t[j][:], func=ACT.Square, accum_out=dist_a[:, col : col + 1])
-
-        def closes_class(j):
-            return 0 <= j < N_JOBS and jobs[j][0] == "C" and jobs[j][2] == 3
-
-        for j in range(N_JOBS):
-            if issue[j] == -1:
-                second_product(j)
+        for j in range(BANKS_C):
+            second_product(j)
         done = 0
-        for j in range(N_JOBS + max(R_LAG, E_LAG, A_LAG) + 1):
+        for j in range(N_JOBS + R_LAG):
             while done < len(pieces) and due(pieces[done]) <= j:
                 kind, k = pieces[done]
                 if kind == "R":
-                    regroup_class(k, "V")
+                    regroup_class(k)
                 else:
                     quant_class(k)
                 done += 1
             if j < N_JOBS:
-                leave_psum(j)
-            for i in range(N_JOBS):
-                if issue[i] == j:
-                    second_product(i)
-            if closes_class(j):
-                sum_tiles(j)
-            if closes_class(j - R_LAG):
-                sum_rest(j - R_LAG)
-            if 0 <= j - E_LAG < N_JOBS and jobs[j - E_LAG][0] == "A":
-                sum_free(j - E_LAG)
+                square(j)
+                cls = j // 4
+                if j + BANKS_C < N_JOBS:
+                    second_product(j + BANKS_C)
+                if cls == NCLS - 1:
+                    if j % 4 == 0:
+                        acc_t[cls] = bank_t()
+                    for bt in range(4):
+                        add_transposed(cls, j % 4, bt, j % 4 == 0 and bt == 0, j % 4 == 3 and bt == 3)
+                elif j % 4 == 3:
+                    acc_t[cls] = bank_t()
+                    for bt in range(4):
+                        for dt in range(4):
+                            add_transposed(cls, dt, bt, dt == 0, dt == 3)
+            if j == N_JOBS - 1:
+                sum_rest(NCLS - 2)
+                sum_rest(NCLS - 1)
+            elif j >= R_LAG and (j - R_LAG) % 4 == 3 and (j - R_LAG) // 4 < NCLS - 2:
+                sum_rest((j - R_LAG) // 4)
 
-        dist = const.tile([P, 4 * NCLS], F32, name="dist")
         kv = const.tile([P, 4 * NCLS], F32, name="kv")
         sh = const.tile([P, 4 * NCLS], F32, name="sh")
         ex = const.tile([P, 4 * NCLS], F32, name="ex")
@@ -408,20 +322,19 @@ def tile_duqhead_pa_kernel(tc, h, W3, b3, class_weight, centroids, out_0, out_1,
         def spread(x):
             return x[:].unsqueeze(2).to_broadcast([P, 4, NCLS])
 
-        nc.vector.tensor_tensor(out=dist[:], in0=dist_c[:], in1=dist_a[:], op=ALU.add)
-        nc.scalar.activation(out=kv[:], in_=dist[:], func=ACT.Exp, scale=SCALE)
-        nc.sync.dma_start(out=out_2.rearrange("(t p) c -> p t c", t=4), in_=by_tile(kv))
         nc.vector.tensor_reduce(out=mn[:], in_=by_tile(dist), axis=AX.X, op=ALU.min)
         nc.vector.tensor_tensor(out=by_tile(sh), in0=by_tile(dist), in1=spread(mn), op=ALU.subtract)
-        nc.scalar.activation(out=km[:], in_=mn[:], func=ACT.Exp, scale=SCALE)
         nc.scalar.activation(out=ex[:], in_=sh[:], func=ACT.Exp, scale=SCALE)
-        nc.vector.tensor_scalar(out=unc[:, 0:4], in0=km[:], scalar1=-1.0, scalar2=1.0, op0=ALU.mult, op1=ALU.add)
-        unc_ps = bank_a()
-        nc.tensor.transpose(unc_ps[:, 0:P], unc[:], ident[:])
+        nc.scalar.activation(out=km[:], in_=mn[:], func=ACT.Exp, scale=SCALE)
+        nc.scalar.activation(out=kv[:], in_=dist[:], func=ACT.Exp, scale=SCALE)
         nc.vector.tensor_reduce(out=ssum[:], in_=by_tile(ex), axis=AX.X, op=ALU.add)
-        nc.scalar.copy(out=unc_t[0:32, :], in_=unc_ps[0:32, 0:P])
-        nc.sync.dma_start(out=out_3.rearrange("(t p) -> t p", t=4), in_=unc_t[0:4, :])
         nc.vector.reciprocal(out=rs[:], in_=ssum[:])
         nc.vector.tensor_tensor(out=by_tile(pr), in0=by_tile(ex), in1=spread(rs), op=ALU.mult)
         nc.sync.dma_start(out=out_0.rearrange("(t p) c -> p t c", t=4), in_=by_tile(pr))
         nc.sync.dma_start(out=out_1.rearrange("o (t p) c -> p (o t) c", t=4), in_=by_tile(pr))
+        nc.sync.dma_start(out=out_2.rearrange("(t p) c -> p t c", t=4), in_=by_tile(kv))
+        nc.vector.tensor_scalar(out=unc[:, 0:4], in0=km[:], scalar1=-1.0, scalar2=1.0, op0=ALU.mult, op1=ALU.add)
+        unc_ps = bank_h()
+        nc.tensor.transpose(unc_ps[:, 0:P], unc[:], ident[:])
+        nc.scalar.copy(out=unc_t[0:32, :], in_=unc_ps[0:32, 0:P])
+        nc.sync.dma_start(out=out_3.rearrange("(t p) -> t p", t=4), in_=unc_t[0:4, :])

@@ -19,11 +19,16 @@ SCALE = -1.0 / (2.0 * LS * LS)
 FLOPS = 2 * B * HIDDEN * E + 2 * B * E * NCLS * E
 
 N_JOBS = 4 * NCLS
+N_A = 6
+PHASE = 4
 BANKS_C = 4
 BANKS_T = 2
 BANKS_H = 2
-R_LAG = 3
+A_LAG = 5
+E_LAG = 4
+R_LAG = 5
 LEAD = 4
+DIF_BUFS = 4
 RAW_BUFS = 12
 GRP_BUFS = 4
 COD_BUFS = 8
@@ -32,8 +37,48 @@ W_SPLIT = 64
 Z_SPLIT = 84
 
 
+def job_list():
+    raw_jobs = []
+    a = 0
+    c = 0
+    for j in range(N_JOBS):
+        if ((j + 1 + PHASE) * 4 * N_A) // N_JOBS > ((j + PHASE) * 4 * N_A) // N_JOBS:
+            raw_jobs.append(("A", a // 4, a % 4))
+            a += 1
+        else:
+            raw_jobs.append(("C", c // 4, c % 4))
+            c += 1
+    number = {}
+    jobs = []
+    for form, r, part in raw_jobs:
+        if (form, r) not in number:
+            number[(form, r)] = len(number)
+        jobs.append((form, number[(form, r)], part))
+    return jobs
+
+
 def tile_duqhead_pa_kernel(tc, h, W3, b3, class_weight, centroids, out_0, out_1, out_2, out_3):
     nc = tc.nc
+    jobs = job_list()
+    first_job = {}
+    form_of = {}
+    for j, (form, cls, part) in enumerate(jobs):
+        if cls not in first_job:
+            first_job[cls] = j
+            form_of[cls] = form
+    a_slot = {}
+    for cls in range(NCLS):
+        if form_of[cls] == "A":
+            a_slot[cls] = len(a_slot)
+    c_jobs = [j for j in range(N_JOBS) if jobs[j][0] == "C"]
+    a_jobs = [j for j in range(N_JOBS) if jobs[j][0] == "A"]
+    issue = {}
+    for i, j in enumerate(c_jobs):
+        issue[j] = -1 if i < BANKS_C else c_jobs[i - BANKS_C]
+    for i, j in enumerate(a_jobs):
+        issue[j] = 0 if i < BANKS_H else a_jobs[i - BANKS_H] + A_LAG
+    last_cls = jobs[N_JOBS - 1][1]
+    assert jobs[N_JOBS - 1][0] == "C" and jobs[N_JOBS - 4][1] == last_cls
 
     with ExitStack() as ctx:
         const = ctx.enter_context(tc.tile_pool(name="const", bufs=1))
@@ -41,6 +86,7 @@ def tile_duqhead_pa_kernel(tc, h, W3, b3, class_weight, centroids, out_0, out_1,
         grp = ctx.enter_context(tc.tile_pool(name="grp", bufs=GRP_BUFS))
         cod = ctx.enter_context(tc.tile_pool(name="cod", bufs=COD_BUFS))
         sqp = ctx.enter_context(tc.tile_pool(name="sqp", bufs=SQ_BUFS))
+        dif = ctx.enter_context(tc.tile_pool(name="dif", bufs=DIF_BUFS))
         ps_c = ctx.enter_context(tc.psum_pool(name="ps_c", bufs=BANKS_C))
         ps_t = ctx.enter_context(tc.psum_pool(name="ps_t", bufs=BANKS_T))
         ps_h = ctx.enter_context(tc.psum_pool(name="ps_h", bufs=BANKS_H))
@@ -76,6 +122,11 @@ def tile_duqhead_pa_kernel(tc, h, W3, b3, class_weight, centroids, out_0, out_1,
         make_identity(nc, ident[:])
         unc = const.tile([P, P], F32, name="unc")
         nc.vector.memset(unc[:], 0.0)
+        centb = const.tile([P, N_A * E], BF16, name="centb")
+        dist_c = const.tile([P, 4 * NCLS], F32, name="dist_c")
+        nc.vector.memset(dist_c[:], 0.0)
+        dist_a = const.tile([P, 4 * NCLS], F32, name="dist_a")
+        nc.vector.memset(dist_a[:], 0.0)
 
         hcodes = const.tile([P, 4 * 512], U32, name="hcodes", align_bytes=64)
         hscales = const.tile([P, 4 * 512], U8, name="hscales", align_bytes=64)
@@ -104,6 +155,9 @@ def tile_duqhead_pa_kernel(tc, h, W3, b3, class_weight, centroids, out_0, out_1,
 
         def load_class(k):
             if k < NCLS:
+                if form_of[k] == "A":
+                    s = a_slot[k]
+                    nc.sync.dma_start(out=centb[:, s * E : (s + 1) * E], in_=centroids[k, :].partition_broadcast(P))
                 t = raw_tile()
                 nc.sync.dma_start(out=t[:], in_=class_weight[k].rearrange("(p j) d -> p (j d)", j=4))
                 raw_c[k] = t
@@ -230,36 +284,63 @@ def tile_duqhead_pa_kernel(tc, h, W3, b3, class_weight, centroids, out_0, out_1,
             kind, k = piece
             if kind == "R" and k > 2:
                 k = k - 1
-            return 4 * k - BANKS_C - LEAD
+            return issue[first_job[k]] - LEAD
 
         acc_t = {}
         bank = {}
         sq_t = {}
 
+        dif_t = {}
+
         def second_product(j):
-            cls = j // 4
-            sl = slice((j % 4) * P, (j % 4 + 1) * P)
-            ps = bank_c()
-            nc.tensor.matmul_mx(
-                out=ps[:],
-                lhsT=codes_c[cls][:, sl].bitcast(FP8X4),
-                lhsT_scale=scales_c[cls][:, sl],
-                rhs=zcodes[:].bitcast(FP8X4),
-                rhs_scale=zscales[:],
-                start=True,
-                stop=True,
-            )
+            form, cls, part = jobs[j]
+            sl = slice(part * P, (part + 1) * P)
+            if form == "C":
+                ps = bank_c()
+                nc.tensor.matmul_mx(
+                    out=ps[:],
+                    lhsT=codes_c[cls][:, sl].bitcast(FP8X4),
+                    lhsT_scale=scales_c[cls][:, sl],
+                    rhs=zcodes[:].bitcast(FP8X4),
+                    rhs_scale=zscales[:],
+                    start=True,
+                    stop=True,
+                )
+            else:
+                ps = bank_h()
+                nc.tensor.matmul_mx(
+                    out=ps[:],
+                    lhsT=zcodes[:, sl].bitcast(FP8X4),
+                    lhsT_scale=zscales[:, sl],
+                    rhs=codes_c[cls][:].bitcast(FP8X4),
+                    rhs_scale=scales_c[cls][:],
+                    start=True,
+                    stop=True,
+                )
             bank[j] = ps
 
-        def square(j):
-            sq = sqp.tile([P, 512], F32, name="sq", tag="sq")
-            nc.scalar.activation(out=sq[:], in_=bank[j][:], func=ACT.Square, bias=negcent[:, j : j + 1], scale=1.0)
-            sq_t[j] = sq
+        def leave_psum(j):
+            form, cls, part = jobs[j]
+            if form == "C":
+                sq = sqp.tile([P, 512], F32, name="sq", tag="sq")
+                col = cls * 4 + part
+                nc.scalar.activation(out=sq[:], in_=bank[j][:], func=ACT.Square, bias=negcent[:, col : col + 1], scale=1.0)
+                sq_t[(cls, part)] = sq
+            else:
+                df = dif.tile([P, 512], F32, name="df", tag="df")
+                s = a_slot[cls]
+                nc.vector.tensor_tensor(out=df[:], in0=bank[j][:], in1=centb[:, s * E : (s + 1) * E], op=ALU.subtract)
+                dif_t[j] = df
+
+        def sum_free(j):
+            form, cls, part = jobs[j]
+            col = part * NCLS + cls
+            nc.scalar.activation(out=dif_t[j][:], in_=dif_t[j][:], func=ACT.Square, accum_out=dist_a[:, col : col + 1])
 
         def add_transposed(cls, dt, bt, start, stop):
             nc.tensor.matmul(
                 out=acc_t[cls][:, bt * P : (bt + 1) * P],
-                lhsT=sq_t[4 * cls + dt][:, bt * P : (bt + 1) * P],
+                lhsT=sq_t[(cls, dt)][:, bt * P : (bt + 1) * P],
                 rhs=ident[:],
                 is_transpose=True,
                 start=start,
@@ -268,16 +349,18 @@ def tile_duqhead_pa_kernel(tc, h, W3, b3, class_weight, centroids, out_0, out_1,
 
         def sum_rest(cls):
             nc.vector.tensor_reduce(
-                out=dist[:].rearrange("p (t c) -> p t c", t=4)[:, :, cls],
+                out=dist_c[:].rearrange("p (t c) -> p t c", t=4)[:, :, cls],
                 in_=acc_t[cls][:].rearrange("p (t q) -> p t q", t=4),
                 axis=AX.X,
                 op=ALU.add,
             )
 
-        for j in range(BANKS_C):
-            second_product(j)
+        for j in range(N_JOBS):
+            if issue[j] == -1:
+                second_product(j)
         done = 0
-        for j in range(N_JOBS + R_LAG):
+        waiting = []
+        for j in range(N_JOBS):
             while done < len(pieces) and due(pieces[done]) <= j:
                 kind, k = pieces[done]
                 if kind == "R":
@@ -285,26 +368,29 @@ def tile_duqhead_pa_kernel(tc, h, W3, b3, class_weight, centroids, out_0, out_1,
                 else:
                     quant_class(k)
                 done += 1
-            if j < N_JOBS:
-                square(j)
-                cls = j // 4
-                if j + BANKS_C < N_JOBS:
-                    second_product(j + BANKS_C)
-                if cls == NCLS - 1:
-                    if j % 4 == 0:
-                        acc_t[cls] = bank_t()
-                    for bt in range(4):
-                        add_transposed(cls, j % 4, bt, j % 4 == 0 and bt == 0, j % 4 == 3 and bt == 3)
-                elif j % 4 == 3:
+            leave_psum(j)
+            for i in range(N_JOBS):
+                if issue[i] == j:
+                    second_product(i)
+            form, cls, part = jobs[j]
+            if cls == last_cls:
+                if part == 0:
                     acc_t[cls] = bank_t()
-                    for bt in range(4):
-                        for dt in range(4):
-                            add_transposed(cls, dt, bt, dt == 0, dt == 3)
-            if j == N_JOBS - 1:
-                sum_rest(NCLS - 2)
-                sum_rest(NCLS - 1)
-            elif j >= R_LAG and (j - R_LAG) % 4 == 3 and (j - R_LAG) // 4 < NCLS - 2:
-                sum_rest((j - R_LAG) // 4)
+                for bt in range(4):
+                    add_transposed(cls, part, bt, part == 0 and bt == 0, part == 3 and bt == 3)
+            elif form == "C" and part == 3:
+                acc_t[cls] = bank_t()
+                for bt in range(4):
+                    for dt in range(4):
+                        add_transposed(cls, dt, bt, dt == 0, dt == 3)
+                waiting.append((j + R_LAG, cls))
+            while len(waiting) > 0 and (waiting[0][0] <= j or j == N_JOBS - 1):
+                sum_rest(waiting[0][1])
+                waiting = waiting[1:]
+            for i in range(N_JOBS):
+                if jobs[i][0] == "A" and (i + E_LAG == j or (j == N_JOBS - 1 and i + E_LAG > j)):
+                    sum_free(i)
+        sum_rest(last_cls)
 
         kv = const.tile([P, 4 * NCLS], F32, name="kv")
         sh = const.tile([P, 4 * NCLS], F32, name="sh")
@@ -322,6 +408,7 @@ def tile_duqhead_pa_kernel(tc, h, W3, b3, class_weight, centroids, out_0, out_1,
         def spread(x):
             return x[:].unsqueeze(2).to_broadcast([P, 4, NCLS])
 
+        nc.vector.tensor_tensor(out=dist[:], in0=dist_c[:], in1=dist_a[:], op=ALU.add)
         nc.vector.tensor_reduce(out=mn[:], in_=by_tile(dist), axis=AX.X, op=ALU.min)
         nc.vector.tensor_tensor(out=by_tile(sh), in0=by_tile(dist), in1=spread(mn), op=ALU.subtract)
         nc.scalar.activation(out=ex[:], in_=sh[:], func=ACT.Exp, scale=SCALE)

from contextlib import ExitStack

import concourse.mybir as mybir
from concourse.masks import make_identity

F32 = mybir.dt.float32
BF16 = mybir.dt.bfloat16
U32 = mybir.dt.uint32
U8 = mybir.dt.uint8
FP8X4 = mybir.dt.float8_e4m3fn_x4
ALU = mybir.AluOpType
ACT = mybir.ActivationFunctionType
AX = mybir.AxisListType

P = 128
B, HIDDEN, E, NCLS = 512, 2048, 512, 32
LS = 0.1
SCALE = -1.0 / (2.0 * LS * LS)
FLOPS = 2 * B * HIDDEN * E + 2 * B * E * NCLS * E

N_JOBS = 4 * NCLS
N_A = 6
PHASE = 4
BANKS_C = 4
BANKS_T = 2
BANKS_H = 2
A_LAG = 5
E_LAG = 4
R_LAG = 5
LEAD = 4
DIF_BUFS = 4
RAW_BUFS = 12
GRP_BUFS = 4
COD_BUFS = 8
SQ_BUFS = 8
W_SPLIT = 64
Z_SPLIT = 84


def job_list():
    raw_jobs = []
    a = 0
    c = 0
    for j in range(N_JOBS):
        if ((j + 1 + PHASE) * 4 * N_A) // N_JOBS > ((j + PHASE) * 4 * N_A) // N_JOBS:
            raw_jobs.append(("A", a // 4, a % 4))
            a += 1
        else:
            raw_jobs.append(("C", c // 4, c % 4))
            c += 1
    number = {}
    jobs = []
    for form, r, part in raw_jobs:
        if (form, r) not in number:
            number[(form, r)] = len(number)
        jobs.append((form, number[(form, r)], part))
    return jobs


def tile_duqhead_pa_kernel(tc, h, W3, b3, class_weight, centroids, out_0, out_1, out_2, out_3):
    nc = tc.nc
    jobs = job_list()
    first_job = {}
    form_of = {}
    for j, (form, cls, part) in enumerate(jobs):
        if cls not in first_job:
            first_job[cls] = j
            form_of[cls] = form
    a_slot = {}
    for cls in range(NCLS):
        if form_of[cls] == "A":
            a_slot[cls] = len(a_slot)
    c_jobs = [j for j in range(N_JOBS) if jobs[j][0] == "C"]
    a_jobs = [j for j in range(N_JOBS) if jobs[j][0] == "A"]
    issue = {}
    for i, j in enumerate(c_jobs):
        issue[j] = -1 if i < BANKS_C else c_jobs[i - BANKS_C]
    for i, j in enumerate(a_jobs):
        issue[j] = 0 if i < BANKS_H else a_jobs[i - BANKS_H] + A_LAG
    last_cls = jobs[N_JOBS - 1][1]
    assert jobs[N_JOBS - 1][0] == "C" and jobs[N_JOBS - 4][1] == last_cls

    with ExitStack() as ctx:
        const = ctx.enter_context(tc.tile_pool(name="const", bufs=1))
        raw = ctx.enter_context(tc.tile_pool(name="raw", bufs=RAW_BUFS))
        grp = ctx.enter_context(tc.tile_pool(name="grp", bufs=GRP_BUFS))
        cod = ctx.enter_context(tc.tile_pool(name="cod", bufs=COD_BUFS))
        sqp = ctx.enter_context(tc.tile_pool(name="sqp", bufs=SQ_BUFS))
        dif = ctx.enter_context(tc.tile_pool(name="dif", bufs=DIF_BUFS))
        ps_c = ctx.enter_context(tc.psum_pool(name="ps_c", bufs=BANKS_C))
        ps_t = ctx.enter_context(tc.psum_pool(name="ps_t", bufs=BANKS_T))
        ps_h = ctx.enter_context(tc.psum_pool(name="ps_h", bufs=BANKS_H))
        ctx.enter_context(tc.manual_schedule())

        def bank_c():
            return ps_c.tile([P, 512], F32, name="bank_c", tag="bank_c")

        def bank_t():
            return ps_t.tile([P, 512], F32, name="bank_t", tag="bank_t")

        def bank_h():
            return ps_h.tile([P, 512], F32, name="bank_h", tag="bank_h")

        def raw_tile():
            return raw.tile([P, 2048], BF16, name="rawt", tag="rawt")

        def grp_tile():
            return grp.tile([P, 2048], BF16, name="grpt", tag="grpt", align_bytes=64)

        def quant(codes, scales, src):
            nc.vector.quantize_mx(out=codes.bitcast(FP8X4), scales=scales, in_=src)

        b3r = const.tile([P, 4], BF16, name="b3r")
        nc.scalar.dma_start(out=b3r[:], in_=b3.rearrange("(m t) -> m t", t=4))
        cent128 = const.tile([P, P], BF16, name="cent128")
        nc.scalar.dma_start(out=cent128[:], in_=centroids.rearrange("c (t p) -> (c t) p", p=P))

        warm = const.tile([P, 2], F32, name="warm")
        nc.vector.memset(warm[:], 0.0)
        nc.scalar.activation(out=warm[:, 1:2], in_=warm[:, 0:1], func=ACT.Exp)
        ident = const.tile([P, P], F32, name="ident")
        make_identity(nc, ident[:])
        unc = const.tile([P, P], F32, name="unc")
        nc.vector.memset(unc[:], 0.0)
        centb = const.tile([P, N_A * E], BF16, name="centb")
        dist_c = const.tile([P, 4 * NCLS], F32, name="dist_c")
        nc.vector.memset(dist_c[:], 0.0)
        dist_a = const.tile([P, 4 * NCLS], F32, name="dist_a")
        nc.vector.memset(dist_a[:], 0.0)

        hcodes = const.tile([P, 4 * 512], U32, name="hcodes", align_bytes=64)
        hscales = const.tile([P, 4 * 512], U8, name="hscales", align_bytes=64)
        wcodes = const.tile([P, 4 * 512], U32, name="wcodes", align_bytes=64)
        wscales = const.tile([P, 4 * 512], U8, name="wscales", align_bytes=64)
        zcodes = const.tile([P, 512], U32, name="zcodes", align_bytes=64)
        zscales = const.tile([P, 512], U8, name="zscales", align_bytes=64)
        z_t = const.tile([P, 4 * 512], BF16, name="z_t")
        dist = const.tile([P, 4 * NCLS], F32, name="dist")

        h_v = h.rearrange("(t p) k -> p t k", t=4)
        raw_h = []
        raw_w = []
        raw_c = {}
        for g in range(4):
            t = raw_tile()
            nc.sync.dma_start(
                out=t[:].rearrange("p (u e n) -> p u e n", u=2, e=2),
                in_=W3[g * 512 : (g + 1) * 512, :].rearrange("(u q e) n -> q u e n", u=2, e=2),
            )
            raw_w.append(t)
        for g in range(4):
            t = raw_tile()
            nc.sync.dma_start(out=t[:].rearrange("p (t k) -> p t k", t=4), in_=h_v[:, :, g * 512 : (g + 1) * 512])
            raw_h.append(t)

        def load_class(k):
            if k < NCLS:
                if form_of[k] == "A":
                    s = a_slot[k]
                    nc.sync.dma_start(out=centb[:, s * E : (s + 1) * E], in_=centroids[k, :].partition_broadcast(P))
                t = raw_tile()
                nc.sync.dma_start(out=t[:], in_=class_weight[k].rearrange("(p j) d -> p (j d)", j=4))
                raw_c[k] = t

        for k in range(RAW_BUFS - 8):
            load_class(k)

        b3f = const.tile([P, 4], F32, name="b3f")
        nc.vector.tensor_copy(out=b3f[:], in_=b3r[:])
        centn = const.tile([P, P], F32, name="centn")
        nc.vector.tensor_scalar(out=centn[:], in0=cent128[:], scalar1=-1.0, scalar2=None, op0=ALU.mult)

        wg = []

        def regroup_w(g):
            wgt = grp_tile()
            wg.append(wgt)
            dst = wgt[:].rearrange("p (t m j) -> p m j t", t=4, j=4)
            src = raw_w[g][:].rearrange("p (j m t) -> p m j t", j=4, t=4)
            nc.vector.tensor_copy(out=dst[:, 0:W_SPLIT], in_=src[:, 0:W_SPLIT])
            nc.scalar.copy(out=dst[:, W_SPLIT:P], in_=src[:, W_SPLIT:P])
            load_class(RAW_BUFS - 8 + g)

        def quant_w(g):
            quant(wcodes[:, g * 512 : (g + 1) * 512], wscales[:, g * 512 : (g + 1) * 512], wg[g][:])

        regroup_w(0)
        for g in range(1, 4):
            regroup_w(g)
            quant_w(g - 1)
        quant_w(3)

        hg = []
        zps = []

        def first_product(g):
            quant(hcodes[:, g * 512 : (g + 1) * 512], hscales[:, g * 512 : (g + 1) * 512], hg[g][:])
            for t in range(4):
                if g == 0:
                    zps.append(bank_c())
                lo = g * 512 + t * P
                nc.tensor.matmul_mx(
                    out=zps[t][:],
                    lhsT=wcodes[:, lo : lo + P].bitcast(FP8X4),
                    lhsT_scale=wscales[:, lo : lo + P],
                    rhs=hcodes[:, g * 512 : (g + 1) * 512].bitcast(FP8X4),
                    rhs_scale=hscales[:, g * 512 : (g + 1) * 512],
                    start=(g == 0),
                    stop=(g == 3),
                )

        for g in range(4):
            h32 = raw_h[g][:].bitcast(F32)
            hgt = grp_tile()
            hg.append(hgt)
            hg32 = hgt[:].bitcast(F32)
            for half in range(2):
                tp = bank_h() if half == 0 else bank_t()
                for u in range(2):
                    for bb in range(2):
                        bt = 2 * half + bb
                        nc.tensor.transpose(
                            tp[:, u * 256 + bb * P : u * 256 + (bb + 1) * P],
                            h32[:, bt * 256 + u * P : bt * 256 + (u + 1) * P],
                            ident[:],
                        )
                dst = hg32[:, half * 512 : (half + 1) * 512].rearrange("p (b u) -> p b u", u=2)
                src = tp[:].rearrange("p (u b) -> p b u", u=2)
                if half == 0 and g == 3:
                    nc.vector.tensor_copy(out=dst, in_=src)
                else:
                    nc.scalar.copy(out=dst, in_=src)
            load_class(RAW_BUFS - 4 + g)
            if g > 0:
                first_product(g - 1)
        tpc = bank_h()
        nc.tensor.transpose(tpc[:, 0:P], centn[:], ident[:])
        first_product(3)

        grp_c = {}
        codes_c = {}
        scales_c = {}

        def regroup_class(k):
            gt = grp_tile()
            grp_c[k] = gt
            dst = gt[:].rearrange("p (c i t) -> p c t i", i=4, t=4)
            src = raw_c[k][:].rearrange("p (t c i) -> p c t i", t=4, i=4)
            nc.vector.tensor_copy(out=dst, in_=src)
            load_class(k + RAW_BUFS)

        def quant_class(k):
            ct = cod.tile([P, 512], U32, name="cwc", tag="cwc", align_bytes=64)
            st = cod.tile([P, 512], U8, name="cws", tag="cws", align_bytes=64)
            codes_c[k] = ct
            scales_c[k] = st
            quant(ct[:], st[:], grp_c[k][:])

        regroup_class(0)
        negcent = const.tile([P, P], F32, name="negcent")
        nc.vector.tensor_copy(out=negcent[:], in_=tpc[:, 0:P])
        quant_class(0)

        for t in range(4):
            dst = z_t[:, t * 512 : (t + 1) * 512]
            if t < 3:
                nc.scalar.activation(out=dst, in_=zps[t][:], func=ACT.Identity, bias=b3f[:, t : t + 1], scale=1.0)
            else:
                nc.vector.tensor_scalar(out=dst, in0=zps[t][:], scalar1=b3f[:, t : t + 1], scalar2=None, op0=ALU.add)
        zg = grp_tile()
        dst = zg[:].rearrange("p (c i t) -> p c t i", i=4, t=4)
        src = z_t[:].rearrange("p (t c i) -> p c t i", t=4, i=4)
        nc.vector.tensor_copy(out=dst[:, 0:Z_SPLIT], in_=src[:, 0:Z_SPLIT])
        nc.scalar.copy(out=dst[:, Z_SPLIT:P], in_=src[:, Z_SPLIT:P])
        quant(zcodes[:], zscales[:], zg[:])

        pieces = [("R", 1), ("Q", 1), ("R", 2)]
        for k in range(3, NCLS):
            pieces.append(("R", k))
            pieces.append(("Q", k - 1))
        pieces.append(("Q", NCLS - 1))

        def due(piece):
            kind, k = piece
            if kind == "R" and k > 2:
                k = k - 1
            return issue[first_job[k]] - LEAD

        acc_t = {}
        bank = {}
        sq_t = {}

        dif_t = {}

        def second_product(j):
            form, cls, part = jobs[j]
            sl = slice(part * P, (part + 1) * P)
            if form == "C":
                ps = bank_c()
                nc.tensor.matmul_mx(
                    out=ps[:],
                    lhsT=codes_c[cls][:, sl].bitcast(FP8X4),
                    lhsT_scale=scales_c[cls][:, sl],
                    rhs=zcodes[:].bitcast(FP8X4),
                    rhs_scale=zscales[:],
                    start=True,
                    stop=True,
                )
            else:
                ps = bank_h()
                nc.tensor.matmul_mx(
                    out=ps[:],
                    lhsT=zcodes[:, sl].bitcast(FP8X4),
                    lhsT_scale=zscales[:, sl],
                    rhs=codes_c[cls][:].bitcast(FP8X4),
                    rhs_scale=scales_c[cls][:],
                    start=True,
                    stop=True,
                )
            bank[j] = ps

        def leave_psum(j):
            form, cls, part = jobs[j]
            if form == "C":
                sq = sqp.tile([P, 512], F32, name="sq", tag="sq")
                col = cls * 4 + part
                nc.scalar.activation(out=sq[:], in_=bank[j][:], func=ACT.Square, bias=negcent[:, col : col + 1], scale=1.0)
                sq_t[(cls, part)] = sq
            else:
                df = dif.tile([P, 512], F32, name="df", tag="df")
                s = a_slot[cls]
                nc.vector.tensor_tensor(out=df[:], in0=bank[j][:], in1=centb[:, s * E : (s + 1) * E], op=ALU.subtract)
                dif_t[j] = df

        def sum_free(j):
            form, cls, part = jobs[j]
            col = part * NCLS + cls
            nc.scalar.activation(out=dif_t[j][:], in_=dif_t[j][:], func=ACT.Square, accum_out=dist_a[:, col : col + 1])

        def add_transposed(cls, dt, bt, start, stop):
            nc.tensor.matmul(
                out=acc_t[cls][:, bt * P : (bt + 1) * P],
                lhsT=sq_t[(cls, dt)][:, bt * P : (bt + 1) * P],
                rhs=ident[:],
                is_transpose=True,
                start=start,
                stop=stop,
            )

        def sum_rest(cls):
            nc.vector.tensor_reduce(
                out=dist_c[:].rearrange("p (t c) -> p t c", t=4)[:, :, cls],
                in_=acc_t[cls][:].rearrange("p (t q) -> p t q", t=4),
                axis=AX.X,
                op=ALU.add,
            )

        for j in range(N_JOBS):
            if issue[j] == -1:
                second_product(j)
        done = 0
        waiting = []
        for j in range(N_JOBS):
            while done < len(pieces) and due(pieces[done]) <= j:
                kind, k = pieces[done]
                if kind == "R":
                    regroup_class(k)
                else:
                    quant_class(k)
                done += 1
            leave_psum(j)
            for i in range(N_JOBS):
                if issue[i] == j:
                    second_product(i)
            form, cls, part = jobs[j]
            if cls == last_cls:
                if part == 0:
                    acc_t[cls] = bank_t()
                for bt in range(4):
                    add_transposed(cls, part, bt, part == 0 and bt == 0, part == 3 and bt == 3)
            elif form == "C" and part == 3:
                acc_t[cls] = bank_t()
                for bt in range(4):
                    for dt in range(4):
                        add_transposed(cls, dt, bt, dt == 0, dt == 3)
                waiting.append((j + R_LAG, cls))
            while len(waiting) > 0 and (waiting[0][0] <= j or j == N_JOBS - 1):
                sum_rest(waiting[0][1])
                waiting = waiting[1:]
            for i in range(N_JOBS):
                if jobs[i][0] == "A" and (i + E_LAG == j or (j == N_JOBS - 1 and i + E_LAG > j)):
                    sum_free(i)
        sum_rest(last_cls)

        kv = const.tile([P, 4 * NCLS], F32, name="kv")
        sh = const.tile([P, 4 * NCLS], F32, name="sh")
        ex = const.tile([P, 4 * NCLS], F32, name="ex")
        pr = const.tile([P, 4 * NCLS], F32, name="pr")
        mn = const.tile([P, 4], F32, name="mn")
        km = const.tile([P, 4], F32, name="km")
        unc_t = const.tile([P, P], F32, name="unc_t")
        ssum = const.tile([P, 4], F32, name="ssum")
        rs = const.tile([P, 4], F32, name="rs")

        def by_tile(x):
            return x[:].rearrange("p (t c) -> p t c", t=4)

        def spread(x):
            return x[:].unsqueeze(2).to_broadcast([P, 4, NCLS])

        nc.vector.tensor_tensor(out=dist[:], in0=dist_c[:], in1=dist_a[:], op=ALU.add)
        nc.vector.tensor_reduce(out=mn[:], in_=by_tile(dist), axis=AX.X, op=ALU.min)
        nc.vector.tensor_tensor(out=by_tile(sh), in0=by_tile(dist), in1=spread(mn), op=ALU.subtract)
        nc.scalar.activation(out=ex[:], in_=sh[:], func=ACT.Exp, scale=SCALE)
        nc.scalar.activation(out=km[:], in_=mn[:], func=ACT.Exp, scale=SCALE)
        nc.scalar.activation(out=kv[:], in_=dist[:], func=ACT.Exp, scale=SCALE)
        nc.vector.tensor_reduce(out=ssum[:], in_=by_tile(ex), axis=AX.X, op=ALU.add)
        nc.vector.reciprocal(out=rs[:], in_=ssum[:])
        nc.vector.tensor_tensor(out=by_tile(pr), in0=by_tile(ex), in1=spread(rs), op=ALU.mult)
        nc.sync.dma_start(out=out_0.rearrange("(t p) c -> p t c", t=4), in_=by_tile(pr))
        nc.sync.dma_start(out=out_1.rearrange("o (t p) c -> p (o t) c", t=4), in_=by_tile(pr))
        nc.sync.dma_start(out=out_2.rearrange("(t p) c -> p t c", t=4), in_=by_tile(kv))
        nc.vector.tensor_scalar(out=unc[:, 0:4], in0=km[:], scalar1=-1.0, scalar2=1.0, op0=ALU.mult, op1=ALU.add)
        unc_ps = bank_h()
        nc.tensor.transpose(unc_ps[:, 0:P], unc[:], ident[:])
        nc.scalar.copy(out=unc_t[0:32, :], in_=unc_ps[0:32, 0:P])
        nc.sync.dma_start(out=out_3.rearrange("(t p) -> t p", t=4), in_=unc_t[0:4, :])
